import numpy as np
import ml_dtypes


def mxq(x, axis, fmt="e4m3"):
    dtype, down = {"e4m3": (ml_dtypes.float8_e4m3fn, 7), "e5m2": (ml_dtypes.float8_e5m2, 14)}[fmt]
    v = np.moveaxis(np.asarray(x, np.float32).astype(ml_dtypes.bfloat16).astype(np.float64), axis, -1)
    blocks = v.reshape(v.shape[:-1] + (-1, 32))
    amax = np.abs(blocks).max(-1, keepdims=True)
    byte = np.maximum(np.where(amax > 0, np.frexp(amax)[1] - 1 + 127, 0) - down, 1)
    scale = np.exp2(byte - 127.0)
    codes = (blocks / scale).astype(np.float32).astype(dtype).astype(np.float64)
    return np.moveaxis((codes * scale).reshape(v.shape), -1, axis)


WIDE = False


def mx_kscale(k):
    if not WIDE:
        return np.ones(k)
    levels = np.array([10, -10, 5, -5, 0])
    a = np.random.permutation(np.resize(levels, k // 512 * 4)).reshape(k // 512, 4)
    idx = np.arange(k)
    return np.exp2(a[idx // 512, idx % 128 // 32])


BF16 = ml_dtypes.bfloat16


def bf(x):
    return np.asarray(x, np.float32).astype(BF16)


def f64(x):
    return np.asarray(x).astype(np.float64)


B, CIN, COUT, T, F, KH, KW, PH, PW = 2, 1024, 128, 512, 4, 3, 3, 1, 1
OT = T + PH + PH - KH + 1


def setup_inputs():
    s = mx_kscale(CIN)
    return {"x": bf(np.random.standard_normal((B, CIN, T, F)) * s[None, :, None, None]),
            "kernel": bf(np.random.standard_normal((COUT, CIN, F, KH, KW)) / np.sqrt(CIN * KH * KW) / s[None, :, None, None, None]),
            "bias": bf(np.random.standard_normal((1, COUT, 1, F)) * 0.5)}


def reference(x, kernel, bias):
    xq = mxq(f64(x).transpose(3, 2, 0, 1).reshape(F, T * B, CIN), 2, "e4m3")
    kt = f64(kernel).transpose(2, 3, 4, 1, 0)
    out = np.zeros((F, OT * B, COUT))
    for m in range(KH):
        for n in range(KW):
            f0, f1 = max(0, PW - n), min(F, F + PW - n)
            t0, t1 = max(0, PH - m), min(OT, T + PH - m)
            p = xq[f0 + n - PW:f1 + n - PW] @ mxq(kt[f0:f1, m, n], 1, "e4m3")
            p = p[:, (t0 + m - PH) * B:(t1 + m - PH) * B]
            out = out + np.pad(p, ((f0, F - f1), (t0 * B, (OT - t1) * B), (0, 0)))
    return out.reshape(F, OT, B, COUT).transpose(2, 3, 1, 0) + f64(bias)

@@ -1,0 +1,149 @@
+from contextlib import ExitStack
+
+import concourse.mybir as mybir
+
+BF16 = mybir.dt.bfloat16
+F32 = mybir.dt.float32
+U32 = mybir.dt.uint32
+U8 = mybir.dt.uint8
+FP8X4 = mybir.dt.float8_e4m3fn_x4
+
+B, CIN, COUT, T, F, KH, KW = 2, 1024, 128, 512, 4, 3, 3
+P = 128
+PACK = 4
+K_PASS = P * PACK
+HALVES = CIN // K_PASS
+TAPS_ALL = F * KH * KW
+
+PLANE = 64
+STEP = T // PLANE
+PLANES = STEP + KH - 1
+HALF_PLANES = PLANES // 2
+PAD = 4
+FRAMES = PAD + T + PAD
+
+O_CHUNK = 32
+TAPS_PER_QUANT = 2
+
+FLOPS = 2 * 30 * B * T * CIN * COUT
+
+
+def tile_svconv2d_pa_t_kernel(tc, x, kernel, bias, out):
+    nc = tc.nc
+
+    taps = [(f, m, n) for f in range(F) for m in range(KH) for n in range(KW) if 0 <= f + n - 1 < F]
+    dram_index = [(f * KH + m) * KW + n for (f, m, n) in taps]
+    runs = []
+    for slot in range(len(taps)):
+        if slot > 0 and dram_index[slot] == dram_index[slot - 1] + 1:
+            runs[-1] = (runs[-1][0], runs[-1][1] + 1)
+        else:
+            runs.append((slot, 1))
+
+    with ExitStack() as ctx:
+        keep = ctx.enter_context(tc.tile_pool(name="keep", bufs=1))
+        raw_k_pool = ctx.enter_context(tc.tile_pool(name="raw_k", bufs=3))
+        grouped_x_pool = ctx.enter_context(tc.tile_pool(name="grouped_x", bufs=4))
+        psum = ctx.enter_context(tc.psum_pool(name="psum", bufs=1))
+
+        k_codes = keep.tile([P, HALVES, len(taps), COUT], U32, align_bytes=64)
+        k_scales = keep.tile([P, HALVES, len(taps), COUT], U8, align_bytes=64)
+        grouped_k = keep.tile([P, len(taps), COUT, PACK], BF16, align_bytes=64)
+        x_codes = keep.tile([P, B, HALVES, F, PLANES * PLANE], U32, align_bytes=64)
+        x_scales = keep.tile([P, B, HALVES, F, PLANES * PLANE], U8, align_bytes=64)
+        raw_x = [keep.tile([P, PACK, FRAMES, F], BF16, name="raw_x%d" % i) for i in range(2)]
+        by_bin = keep.tile([P, F, T], F32)
+        result = keep.tile([P, T, F], F32)
+        acc = [[psum.tile([P, T], F32, name="acc_%d_%d" % (b, f)) for f in range(F)] for b in range(B)]
+
+        bias_bf16 = keep.tile([P, F], BF16)
+        nc.scalar.dma_start(out=bias_bf16[:], in_=bias[0, :, 0, :])
+        bias_f32 = keep.tile([P, F], F32)
+        nc.vector.tensor_copy(out=bias_f32[:], in_=bias_bf16[:])
+
+        for raw in raw_x:
+            nc.vector.memset(raw[:, :, 0:PAD, :], 0.0)
+            nc.vector.memset(raw[:, :, PAD + T : FRAMES, :], 0.0)
+
+        def load_and_quantise_kernel(c):
+            channels = slice(c * K_PASS, (c + 1) * K_PASS)
+            for chunk in range(COUT // O_CHUNK):
+                o_range = slice(chunk * O_CHUNK, (chunk + 1) * O_CHUNK)
+                raw_k = raw_k_pool.tile([P, O_CHUNK, PACK * TAPS_ALL], BF16)
+                nc.sync.dma_start(
+                    out=raw_k[:],
+                    in_=kernel[o_range, channels].rearrange("o (p j) f m n -> p o (j f m n)", j=PACK),
+                )
+                by_tap = raw_k[:].rearrange("p o (j r) -> p r o j", j=PACK)
+                for first_slot, count in runs:
+                    first = dram_index[first_slot]
+                    dst = grouped_k[:, first_slot : first_slot + count, o_range, :]
+                    src = by_tap[:, first : first + count]
+                    if chunk % 2 == 0:
+                        nc.vector.tensor_copy(out=dst, in_=src)
+                    else:
+                        nc.scalar.copy(out=dst, in_=src)
+            for slot in range(0, len(taps), TAPS_PER_QUANT):
+                slots = slice(slot, slot + TAPS_PER_QUANT)
+                nc.vector.quantize_mx(
+                    out=k_codes[:, c, slots, :].rearrange("p s o -> p (s o)").bitcast(FP8X4),
+                    scales=k_scales[:, c, slots, :].rearrange("p s o -> p (s o)"),
+                    in_=grouped_k[:, slots].rearrange("p s o j -> p (s o j)"),
+                )
+
+        def load_and_quantise_x(b, c, raw):
+            channels = slice(c * K_PASS, (c + 1) * K_PASS)
+            nc.sync.dma_start(
+                out=raw[:, :, PAD : PAD + T, :],
+                in_=x[b, channels].rearrange("(p j) t f -> p j t f", j=PACK),
+            )
+            for f in range(F):
+                grouped_x = grouped_x_pool.tile([P, PLANES, PLANE, PACK], BF16, align_bytes=64)
+                low = raw[:, :, 0:T, f].rearrange("p j (q r) -> p r q j", r=STEP)
+                high = raw[:, :, STEP : STEP + T, f].rearrange("p j (q r) -> p r q j", r=STEP)
+                nc.vector.tensor_copy(out=grouped_x[:, 0:HALF_PLANES], in_=low[:, PAD - 1 : STEP])
+                nc.scalar.copy(out=grouped_x[:, HALF_PLANES:PLANES], in_=high[:, 0:HALF_PLANES])
+                flat = grouped_x[:].rearrange("p l q j -> p (l q j)")
+                for first, width in ((0, 512), (512, 128)):
+                    nc.vector.quantize_mx(
+                        out=x_codes[:, b, c, f, first : first + width].bitcast(FP8X4),
+                        scales=x_scales[:, b, c, f, first : first + width],
+                        in_=flat[:, PACK * first : PACK * (first + width)],
+                    )
+
+        def multiply(b, c):
+            for slot, (f, m, n) in enumerate(taps):
+                window = slice(m * PLANE, m * PLANE + T)
+                nc.tensor.matmul_mx(
+                    out=acc[b][f][:],
+                    lhsT=k_codes[:, c, slot, :].bitcast(FP8X4),
+                    lhsT_scale=k_scales[:, c, slot, :],
+                    rhs=x_codes[:, b, c, f + n - 1, window].bitcast(FP8X4),
+                    rhs_scale=x_scales[:, b, c, f + n - 1, window],
+                    start=(c == 0 and (slot == 0 or taps[slot - 1][0] != f)),
+                    stop=(c == HALVES - 1 and (slot == len(taps) - 1 or taps[slot + 1][0] != f)),
+                )
+
+        def store(b):
+            for f in range(F):
+                nc.scalar.activation(
+                    out=by_bin[:, f, :].rearrange("p (q r) -> p q r", r=STEP),
+                    in_=acc[b][f][:].rearrange("p (r q) -> p q r", r=STEP),
+                    func=mybir.ActivationFunctionType.Identity,
+                    bias=bias_f32[:, f : f + 1],
+                )
+            nc.vector.tensor_copy(out=result[:], in_=by_bin[:].rearrange("p f t -> p t f"))
+            nc.sync.dma_start(out=out[b].rearrange("o t f -> o (t f)"), in_=result[:].rearrange("p t f -> p (t f)"))
+
+        load_and_quantise_kernel(0)
+        load_and_quantise_x(0, 0, raw_x[0])
+        load_and_quantise_x(1, 0, raw_x[1])
+        multiply(0, 0)
+        multiply(1, 0)
+        load_and_quantise_x(0, 1, raw_x[0])
+        load_and_quantise_kernel(1)
+        load_and_quantise_x(1, 1, raw_x[1])
+        multiply(0, 1)
+        store(0)
+        multiply(1, 1)
+        store(1)

@@ -18,12 +18,11 @@ TAPS_ALL = F * KH * KW
 PLANE = 64
 STEP = T // PLANE
 PLANES = STEP + KH - 1
-HALF_PLANES = PLANES // 2
 PAD = 4
 FRAMES = PAD + T + PAD
 
 O_CHUNK = 32
-TAPS_PER_QUANT = 2
+TAPS_PER_COPY = 4
 
 FLOPS = 2 * 30 * B * T * CIN * COUT
 
@@ -32,28 +31,17 @@ def tile_svconv2d_pa_t_kernel(tc, x, kernel, bias, out):
     nc = tc.nc
 
     taps = [(f, m, n) for f in range(F) for m in range(KH) for n in range(KW) if 0 <= f + n - 1 < F]
-    dram_index = [(f * KH + m) * KW + n for (f, m, n) in taps]
-    runs = []
-    for slot in range(len(taps)):
-        if slot > 0 and dram_index[slot] == dram_index[slot - 1] + 1:
-            runs[-1] = (runs[-1][0], runs[-1][1] + 1)
-        else:
-            runs.append((slot, 1))
 
     with ExitStack() as ctx:
         keep = ctx.enter_context(tc.tile_pool(name="keep", bufs=1))
-        raw_k_pool = ctx.enter_context(tc.tile_pool(name="raw_k", bufs=3))
-        grouped_x_pool = ctx.enter_context(tc.tile_pool(name="grouped_x", bufs=4))
+        grouped_x_pool = ctx.enter_context(tc.tile_pool(name="grouped_x", bufs=2))
         psum = ctx.enter_context(tc.psum_pool(name="psum", bufs=1))
 
         k_codes = keep.tile([P, HALVES, len(taps), COUT], U32, align_bytes=64)
         k_scales = keep.tile([P, HALVES, len(taps), COUT], U8, align_bytes=64)
-        grouped_k = keep.tile([P, len(taps), COUT, PACK], BF16, align_bytes=64)
         x_codes = keep.tile([P, B, HALVES, F, PLANES * PLANE], U32, align_bytes=64)
         x_scales = keep.tile([P, B, HALVES, F, PLANES * PLANE], U8, align_bytes=64)
         raw_x = [keep.tile([P, PACK, FRAMES, F], BF16, name="raw_x%d" % i) for i in range(2)]
-        by_bin = keep.tile([P, F, T], F32)
-        result = keep.tile([P, T, F], F32)
         acc = [[psum.tile([P, T], F32, name="acc_%d_%d" % (b, f)) for f in range(F)] for b in range(B)]
 
         bias_bf16 = keep.tile([P, F], BF16)
@@ -65,7 +53,7 @@ def tile_svconv2d_pa_t_kernel(tc, x, kernel, bias, out):
             nc.vector.memset(raw[:, :, 0:PAD, :], 0.0)
             nc.vector.memset(raw[:, :, PAD + T : FRAMES, :], 0.0)
 
-        def load_and_quantise_kernel(c):
+        def load_and_quantise_kernel(c, raw_k_pool, grouped_k):
             channels = slice(c * K_PASS, (c + 1) * K_PASS)
             for chunk in range(COUT // O_CHUNK):
                 o_range = slice(chunk * O_CHUNK, (chunk + 1) * O_CHUNK)
@@ -74,21 +62,19 @@ def tile_svconv2d_pa_t_kernel(tc, x, kernel, bias, out):
                     out=raw_k[:],
                     in_=kernel[o_range, channels].rearrange("o (p j) f m n -> p o (j f m n)", j=PACK),
                 )
-                by_tap = raw_k[:].rearrange("p o (j r) -> p r o j", j=PACK)
-                for first_slot, count in runs:
-                    first = dram_index[first_slot]
-                    dst = grouped_k[:, first_slot : first_slot + count, o_range, :]
-                    src = by_tap[:, first : first + count]
+                for first in range(0, TAPS_ALL, TAPS_PER_COPY):
+                    four_taps = slice(first, first + TAPS_PER_COPY)
+                    dst = grouped_k[:, four_taps, o_range, :].rearrange("p r o j -> p o j r")
+                    src = raw_k[:].rearrange("p o (j r) -> p o j r", j=PACK)[:, :, :, four_taps]
                     if chunk % 2 == 0:
                         nc.vector.tensor_copy(out=dst, in_=src)
                     else:
                         nc.scalar.copy(out=dst, in_=src)
-            for slot in range(0, len(taps), TAPS_PER_QUANT):
-                slots = slice(slot, slot + TAPS_PER_QUANT)
+            for slot, (f, m, n) in enumerate(taps):
                 nc.vector.quantize_mx(
-                    out=k_codes[:, c, slots, :].rearrange("p s o -> p (s o)").bitcast(FP8X4),
-                    scales=k_scales[:, c, slots, :].rearrange("p s o -> p (s o)"),
-                    in_=grouped_k[:, slots].rearrange("p s o j -> p (s o j)"),
+                    out=k_codes[:, c, slot, :].bitcast(FP8X4),
+                    scales=k_scales[:, c, slot, :],
+                    in_=grouped_k[:, (f * KH + m) * KW + n].rearrange("p o j -> p (o j)"),
                 )
 
         def load_and_quantise_x(b, c, raw):
@@ -97,13 +83,17 @@ def tile_svconv2d_pa_t_kernel(tc, x, kernel, bias, out):
                 out=raw[:, :, PAD : PAD + T, :],
                 in_=x[b, channels].rearrange("(p j) t f -> p j t f", j=PACK),
             )
+            grouped_x = grouped_x_pool.tile([P, F, PLANES, PLANE, PACK], BF16, align_bytes=64)
+            for plane in range(PLANES):
+                first = plane + PAD - 1
+                dst = grouped_x[:, :, plane].rearrange("p f q j -> p q j f")
+                src = raw[:, :, first : first + STEP * (PLANE - 1) + 1 : STEP, :].rearrange("p j q f -> p q j f")
+                if plane % 2 == 0:
+                    nc.vector.tensor_copy(out=dst, in_=src)
+                else:
+                    nc.scalar.copy(out=dst, in_=src)
             for f in range(F):
-                grouped_x = grouped_x_pool.tile([P, PLANES, PLANE, PACK], BF16, align_bytes=64)
-                low = raw[:, :, 0:T, f].rearrange("p j (q r) -> p r q j", r=STEP)
-                high = raw[:, :, STEP : STEP + T, f].rearrange("p j (q r) -> p r q j", r=STEP)
-                nc.vector.tensor_copy(out=grouped_x[:, 0:HALF_PLANES], in_=low[:, PAD - 1 : STEP])
-                nc.scalar.copy(out=grouped_x[:, HALF_PLANES:PLANES], in_=high[:, 0:HALF_PLANES])
-                flat = grouped_x[:].rearrange("p l q j -> p (l q j)")
+                flat = grouped_x[:, f].rearrange("p l q j -> p (l q j)")
                 for first, width in ((0, 512), (512, 128)):
                     nc.vector.quantize_mx(
                         out=x_codes[:, b, c, f, first : first + width].bitcast(FP8X4),
@@ -124,7 +114,7 @@ def tile_svconv2d_pa_t_kernel(tc, x, kernel, bias, out):
                     stop=(c == HALVES - 1 and (slot == len(taps) - 1 or taps[slot + 1][0] != f)),
                 )
 
-        def store(b):
+        def store(b, by_bin, result):
             for f in range(F):
                 nc.scalar.activation(
                     out=by_bin[:, f, :].rearrange("p (q r) -> p q r", r=STEP),
@@ -135,15 +125,20 @@ def tile_svconv2d_pa_t_kernel(tc, x, kernel, bias, out):
             nc.vector.tensor_copy(out=result[:], in_=by_bin[:].rearrange("p f t -> p t f"))
             nc.sync.dma_start(out=out[b].rearrange("o t f -> o (t f)"), in_=result[:].rearrange("p t f -> p (t f)"))
 
-        load_and_quantise_kernel(0)
-        load_and_quantise_x(0, 0, raw_x[0])
-        load_and_quantise_x(1, 0, raw_x[1])
-        multiply(0, 0)
-        multiply(1, 0)
-        load_and_quantise_x(0, 1, raw_x[0])
-        load_and_quantise_kernel(1)
+        with tc.tile_pool(name="raw_k", bufs=3) as raw_k_pool, tc.tile_pool(name="grouped_k", bufs=1) as grouped_k_pool:
+            grouped_k = grouped_k_pool.tile([P, TAPS_ALL, COUT, PACK], BF16, align_bytes=64)
+            load_and_quantise_kernel(0, raw_k_pool, grouped_k)
+            load_and_quantise_x(0, 0, raw_x[0])
+            load_and_quantise_x(1, 0, raw_x[1])
+            multiply(0, 0)
+            multiply(1, 0)
+            load_and_quantise_x(0, 1, raw_x[0])
+            load_and_quantise_kernel(1, raw_k_pool, grouped_k)
         load_and_quantise_x(1, 1, raw_x[1])
-        multiply(0, 1)
-        store(0)
-        multiply(1, 1)
-        store(1)
+        with tc.tile_pool(name="results", bufs=1) as results:
+            by_bin = results.tile([P, F, T], F32)
+            result = results.tile([P, T, F], F32)
+            multiply(0, 1)
+            store(0, by_bin, result)
+            multiply(1, 1)
+            store(1, by_bin, result)

@@ -67,9 +67,9 @@ def tile_svconv2d_pa_t_kernel(tc, x, kernel, bias, out):
                     dst = grouped_k[:, four_taps, o_range, :].rearrange("p r o j -> p o j r")
                     src = raw_k[:].rearrange("p o (j r) -> p o j r", j=PACK)[:, :, :, four_taps]
                     if chunk % 2 == 0:
-                        nc.vector.tensor_copy(out=dst, in_=src)
-                    else:
                         nc.scalar.copy(out=dst, in_=src)
+                    else:
+                        nc.vector.tensor_copy(out=dst, in_=src)
             for slot, (f, m, n) in enumerate(taps):
                 nc.vector.quantize_mx(
                     out=k_codes[:, c, slot, :].bitcast(FP8X4),
@@ -88,10 +88,10 @@ def tile_svconv2d_pa_t_kernel(tc, x, kernel, bias, out):
                 first = plane + PAD - 1
                 dst = grouped_x[:, :, plane].rearrange("p f q j -> p q j f")
                 src = raw[:, :, first : first + STEP * (PLANE - 1) + 1 : STEP, :].rearrange("p j q f -> p q j f")
-                if plane % 2 == 0:
-                    nc.vector.tensor_copy(out=dst, in_=src)
-                else:
+                if plane % 3 == 2:
                     nc.scalar.copy(out=dst, in_=src)
+                else:
+                    nc.vector.tensor_copy(out=dst, in_=src)
             for f in range(F):
                 flat = grouped_x[:, f].rearrange("p l q j -> p (l q j)")
                 for first, width in ((0, 512), (512, 128)):
@@ -122,8 +122,14 @@ def tile_svconv2d_pa_t_kernel(tc, x, kernel, bias, out):
                     func=mybir.ActivationFunctionType.Identity,
                     bias=bias_f32[:, f : f + 1],
                 )
-            nc.vector.tensor_copy(out=result[:], in_=by_bin[:].rearrange("p f t -> p t f"))
-            nc.sync.dma_start(out=out[b].rearrange("o t f -> o (t f)"), in_=result[:].rearrange("p t f -> p (t f)"))
+            early, late = slice(0, T // 2), slice(T // 2, T)
+            nc.vector.tensor_copy(out=result[:, early, :], in_=by_bin[:, :, early].rearrange("p f t -> p t f"))
+            nc.scalar.copy(out=result[:, late, :], in_=by_bin[:, :, late].rearrange("p f t -> p t f"))
+            for frames in (early, late):
+                nc.sync.dma_start(
+                    out=out[b, :, frames, :].rearrange("o t f -> o (t f)"),
+                    in_=result[:, frames, :].rearrange("p t f -> p (t f)"),
+                )
 
         with tc.tile_pool(name="raw_k", bufs=3) as raw_k_pool, tc.tile_pool(name="grouped_k", bufs=1) as grouped_k_pool:
             grouped_k = grouped_k_pool.tile([P, TAPS_ALL, COUT, PACK], BF16, align_bytes=64)

@@ -1,6 +1,7 @@
 from contextlib import ExitStack
 
 import concourse.mybir as mybir
+from concourse.masks import make_identity
 
 BF16 = mybir.dt.bfloat16
 F32 = mybir.dt.float32
@@ -14,6 +15,8 @@ PACK = 4
 K_PASS = P * PACK
 HALVES = CIN // K_PASS
 TAPS_ALL = F * KH * KW
+TAP_PAIRS = TAPS_ALL // 2
+BANKS = 8
 
 PLANE = 64
 STEP = T // PLANE
@@ -31,6 +34,7 @@ def tile_svconv2d_pa_t_kernel(tc, x, kernel, bias, out):
     nc = tc.nc
 
     taps = [(f, m, n) for f in range(F) for m in range(KH) for n in range(KW) if 0 <= f + n - 1 < F]
+    places = [(f * KH + m) * KW + n for f, m, n in taps]
 
     with ExitStack() as ctx:
         keep = ctx.enter_context(tc.tile_pool(name="keep", bufs=1))
@@ -42,7 +46,9 @@ def tile_svconv2d_pa_t_kernel(tc, x, kernel, bias, out):
         x_codes = keep.tile([P, B, HALVES, F, PLANES * PLANE], U32, align_bytes=64)
         x_scales = keep.tile([P, B, HALVES, F, PLANES * PLANE], U8, align_bytes=64)
         raw_x = [keep.tile([P, PACK, FRAMES, F], BF16, name="raw_x%d" % i) for i in range(2)]
-        acc = [[psum.tile([P, T], F32, name="acc_%d_%d" % (b, f)) for f in range(F)] for b in range(B)]
+
+        identity = keep.tile([P, P], F32)
+        make_identity(nc, identity[:])
 
         bias_bf16 = keep.tile([P, F], BF16)
         nc.scalar.dma_start(out=bias_bf16[:], in_=bias[0, :, 0, :])
@@ -53,11 +59,38 @@ def tile_svconv2d_pa_t_kernel(tc, x, kernel, bias, out):
             nc.vector.memset(raw[:, :, 0:PAD, :], 0.0)
             nc.vector.memset(raw[:, :, PAD + T : FRAMES, :], 0.0)
 
-        def load_and_quantise_kernel(c, raw_k_pool, grouped_k):
+        def quantise_kernel(c, grouped_k):
+            for slot, place in enumerate(places):
+                nc.vector.quantize_mx(
+                    out=k_codes[:, c, slot, :].bitcast(FP8X4),
+                    scales=k_scales[:, c, slot, :],
+                    in_=grouped_k[:, place].rearrange("p o j -> p (o j)"),
+                )
+
+        def kernel_by_transposes(c, whole_pool, grouped_k):
+            channels = slice(c * K_PASS, (c + 1) * K_PASS)
+            by_output = whole_pool.tile([P, K_PASS * TAPS_ALL], BF16)
+            nc.sync.dma_start(out=by_output[:], in_=kernel[:, channels].rearrange("o i f m n -> o (i f m n)"))
+            words = by_output[:].bitcast(F32).rearrange("o (p j w) -> o p j w", j=PACK, w=TAP_PAIRS)
+            for w in range(TAP_PAIRS):
+                turned = psum.tile([P, PACK * COUT], F32, name="turned%d" % w, tag="bank%d" % (w % BANKS))
+                for j in range(PACK):
+                    nc.tensor.transpose(turned[:, j * COUT : (j + 1) * COUT], words[:, :, j, w], identity[:])
+                wanted = [e for e in range(2) if 2 * w + e in places]
+                halves = slice(wanted[0], wanted[-1] + 1)
+                dst = grouped_k[:, 2 * w : 2 * w + 2].rearrange("p e o j -> p o j e")[:, :, :, halves]
+                src = turned[:].bitcast(BF16).rearrange("p (j o e) -> p o j e", j=PACK, e=2)[:, :, :, halves]
+                if w % 3 == 0:
+                    nc.vector.tensor_copy(out=dst, in_=src)
+                else:
+                    nc.scalar.copy(out=dst, in_=src)
+            quantise_kernel(c, grouped_k)
+
+        def kernel_in_short_runs(c, chunk_pool, grouped_k):
             channels = slice(c * K_PASS, (c + 1) * K_PASS)
             for chunk in range(COUT // O_CHUNK):
                 o_range = slice(chunk * O_CHUNK, (chunk + 1) * O_CHUNK)
-                raw_k = raw_k_pool.tile([P, O_CHUNK, PACK * TAPS_ALL], BF16)
+                raw_k = chunk_pool.tile([P, O_CHUNK, PACK * TAPS_ALL], BF16)
                 nc.sync.dma_start(
                     out=raw_k[:],
                     in_=kernel[o_range, channels].rearrange("o (p j) f m n -> p o (j f m n)", j=PACK),
@@ -70,12 +103,7 @@ def tile_svconv2d_pa_t_kernel(tc, x, kernel, bias, out):
                         nc.scalar.copy(out=dst, in_=src)
                     else:
                         nc.vector.tensor_copy(out=dst, in_=src)
-            for slot, (f, m, n) in enumerate(taps):
-                nc.vector.quantize_mx(
-                    out=k_codes[:, c, slot, :].bitcast(FP8X4),
-                    scales=k_scales[:, c, slot, :],
-                    in_=grouped_k[:, (f * KH + m) * KW + n].rearrange("p o j -> p (o j)"),
-                )
+            quantise_kernel(c, grouped_k)
 
         def load_and_quantise_x(b, c, raw):
             channels = slice(c * K_PASS, (c + 1) * K_PASS)
@@ -101,7 +129,7 @@ def tile_svconv2d_pa_t_kernel(tc, x, kernel, bias, out):
                         in_=flat[:, PACK * first : PACK * (first + width)],
                     )
 
-        def multiply(b, c):
+        def multiply(b, c, acc):
             for slot, (f, m, n) in enumerate(taps):
                 window = slice(m * PLANE, m * PLANE + T)
                 nc.tensor.matmul_mx(
@@ -114,7 +142,7 @@ def tile_svconv2d_pa_t_kernel(tc, x, kernel, bias, out):
                     stop=(c == HALVES - 1 and (slot == len(taps) - 1 or taps[slot + 1][0] != f)),
                 )
 
-        def store(b, by_bin, result):
+        def store(b, acc, by_bin, result):
             for f in range(F):
                 nc.scalar.activation(
                     out=by_bin[:, f, :].rearrange("p (q r) -> p q r", r=STEP),
@@ -122,29 +150,29 @@ def tile_svconv2d_pa_t_kernel(tc, x, kernel, bias, out):
                     func=mybir.ActivationFunctionType.Identity,
                     bias=bias_f32[:, f : f + 1],
                 )
-            early, late = slice(0, T // 2), slice(T // 2, T)
-            nc.vector.tensor_copy(out=result[:, early, :], in_=by_bin[:, :, early].rearrange("p f t -> p t f"))
-            nc.scalar.copy(out=result[:, late, :], in_=by_bin[:, :, late].rearrange("p f t -> p t f"))
-            for frames in (early, late):
-                nc.sync.dma_start(
-                    out=out[b, :, frames, :].rearrange("o t f -> o (t f)"),
-                    in_=result[:, frames, :].rearrange("p t f -> p (t f)"),
-                )
+            nc.vector.tensor_copy(out=result[:], in_=by_bin[:].rearrange("p f t -> p t f"))
+            nc.sync.dma_start(out=out[b].rearrange("o t f -> o (t f)"), in_=result[:].rearrange("p t f -> p (t f)"))
 
-        with tc.tile_pool(name="raw_k", bufs=3) as raw_k_pool, tc.tile_pool(name="grouped_k", bufs=1) as grouped_k_pool:
+        with tc.tile_pool(name="grouped_k", bufs=1) as grouped_k_pool:
             grouped_k = grouped_k_pool.tile([P, TAPS_ALL, COUT, PACK], BF16, align_bytes=64)
-            load_and_quantise_kernel(0, raw_k_pool, grouped_k)
             load_and_quantise_x(0, 0, raw_x[0])
+            with tc.tile_pool(name="whole", bufs=1) as whole_pool:
+                kernel_by_transposes(0, whole_pool, grouped_k)
             load_and_quantise_x(1, 0, raw_x[1])
-            multiply(0, 0)
-            multiply(1, 0)
+            acc = [
+                [psum.tile([P, T], F32, name="acc_%d_%d" % (b, f), tag="bank%d" % (b * F + f)) for f in range(F)]
+                for b in range(B)
+            ]
+            multiply(0, 0, acc)
+            multiply(1, 0, acc)
             load_and_quantise_x(0, 1, raw_x[0])
-            load_and_quantise_kernel(1, raw_k_pool, grouped_k)
+            with tc.tile_pool(name="chunks", bufs=3) as chunk_pool:
+                kernel_in_short_runs(1, chunk_pool, grouped_k)
         load_and_quantise_x(1, 1, raw_x[1])
         with tc.tile_pool(name="results", bufs=1) as results:
             by_bin = results.tile([P, F, T], F32)
             result = results.tile([P, T, F], F32)
-            multiply(0, 1)
-            store(0, by_bin, result)
-            multiply(1, 1)
-            store(1, by_bin, result)
+            multiply(0, 1, acc)
+            store(0, acc, by_bin, result)
+            multiply(1, 1, acc)
+            store(1, acc, by_bin, result)

@@ -38,14 +38,21 @@ def tile_svconv2d_pa_t_kernel(tc, x, kernel, bias, out):
 
     with ExitStack() as ctx:
         keep = ctx.enter_context(tc.tile_pool(name="keep", bufs=1))
+        raw_x_pool = ctx.enter_context(tc.tile_pool(name="raw_x", bufs=2))
         grouped_x_pool = ctx.enter_context(tc.tile_pool(name="grouped_x", bufs=2))
+        grouped_k_pool = ctx.enter_context(tc.tile_pool(name="grouped_k", bufs=1))
+        chunk_pool = ctx.enter_context(tc.tile_pool(name="chunks", bufs=COUT // O_CHUNK))
         psum = ctx.enter_context(tc.psum_pool(name="psum", bufs=1))
 
-        k_codes = keep.tile([P, HALVES, len(taps), COUT], U32, align_bytes=64)
-        k_scales = keep.tile([P, HALVES, len(taps), COUT], U8, align_bytes=64)
-        x_codes = keep.tile([P, B, HALVES, F, PLANES * PLANE], U32, align_bytes=64)
-        x_scales = keep.tile([P, B, HALVES, F, PLANES * PLANE], U8, align_bytes=64)
-        raw_x = [keep.tile([P, PACK, FRAMES, F], BF16, name="raw_x%d" % i) for i in range(2)]
+        def quantised_half(pool, c):
+            return {
+                "k_codes": pool.tile([P, len(taps), COUT], U32, name="k_codes%d" % c, align_bytes=64),
+                "k_scales": pool.tile([P, len(taps), COUT], U8, name="k_scales%d" % c, align_bytes=64),
+                "x_codes": pool.tile([P, B, F, PLANES * PLANE], U32, name="x_codes%d" % c, align_bytes=64),
+                "x_scales": pool.tile([P, B, F, PLANES * PLANE], U8, name="x_scales%d" % c, align_bytes=64),
+            }
+
+        grouped_k = grouped_k_pool.tile([P, TAPS_ALL, COUT, PACK], BF16, align_bytes=64)
 
         identity = keep.tile([P, P], F32)
         make_identity(nc, identity[:])
@@ -55,94 +62,96 @@ def tile_svconv2d_pa_t_kernel(tc, x, kernel, bias, out):
         bias_f32 = keep.tile([P, F], F32)
         nc.vector.tensor_copy(out=bias_f32[:], in_=bias_bf16[:])
 
-        for raw in raw_x:
+        def load_x(b, c):
+            raw = raw_x_pool.tile([P, PACK, FRAMES, F], BF16, name="raw_x_%d_%d" % (b, c), tag="raw_x")
             nc.vector.memset(raw[:, :, 0:PAD, :], 0.0)
             nc.vector.memset(raw[:, :, PAD + T : FRAMES, :], 0.0)
+            nc.sync.dma_start(
+                out=raw[:, :, PAD : PAD + T, :],
+                in_=x[b, c * K_PASS : (c + 1) * K_PASS].rearrange("(p j) t f -> p j t f", j=PACK),
+            )
+            return raw
 
-        def quantise_kernel(c, grouped_k):
+        def quantise_x(b, raw, half):
+            grouped_x = grouped_x_pool.tile([P, F, PLANES, PLANE, PACK], BF16, align_bytes=64)
+            for plane in range(PLANES):
+                first = plane + PAD - 1
+                dst = grouped_x[:, :, plane].rearrange("p f q j -> p q j f")
+                src = raw[:, :, first : first + STEP * (PLANE - 1) + 1 : STEP, :].rearrange("p j q f -> p q j f")
+                if plane % 2 == 0:
+                    nc.vector.tensor_copy(out=dst, in_=src)
+                else:
+                    nc.scalar.copy(out=dst, in_=src)
+            for f in range(F):
+                flat = grouped_x[:, f].rearrange("p l q j -> p (l q j)")
+                for first, width in ((0, 512), (512, 128)):
+                    nc.vector.quantize_mx(
+                        out=half["x_codes"][:, b, f, first : first + width].bitcast(FP8X4),
+                        scales=half["x_scales"][:, b, f, first : first + width],
+                        in_=flat[:, PACK * first : PACK * (first + width)],
+                    )
+
+        def quantise_kernel(half):
             for slot, place in enumerate(places):
                 nc.vector.quantize_mx(
-                    out=k_codes[:, c, slot, :].bitcast(FP8X4),
-                    scales=k_scales[:, c, slot, :],
+                    out=half["k_codes"][:, slot, :].bitcast(FP8X4),
+                    scales=half["k_scales"][:, slot, :],
                     in_=grouped_k[:, place].rearrange("p o j -> p (o j)"),
                 )
 
-        def kernel_by_transposes(c, whole_pool, grouped_k):
-            channels = slice(c * K_PASS, (c + 1) * K_PASS)
-            by_output = whole_pool.tile([P, K_PASS * TAPS_ALL], BF16)
-            nc.sync.dma_start(out=by_output[:], in_=kernel[:, channels].rearrange("o i f m n -> o (i f m n)"))
+        def turn_kernel(by_output):
             words = by_output[:].bitcast(F32).rearrange("o (p j w) -> o p j w", j=PACK, w=TAP_PAIRS)
             for w in range(TAP_PAIRS):
                 turned = psum.tile([P, PACK * COUT], F32, name="turned%d" % w, tag="bank%d" % (w % BANKS))
                 for j in range(PACK):
                     nc.tensor.transpose(turned[:, j * COUT : (j + 1) * COUT], words[:, :, j, w], identity[:])
                 wanted = [e for e in range(2) if 2 * w + e in places]
-                halves = slice(wanted[0], wanted[-1] + 1)
-                dst = grouped_k[:, 2 * w : 2 * w + 2].rearrange("p e o j -> p o j e")[:, :, :, halves]
-                src = turned[:].bitcast(BF16).rearrange("p (j o e) -> p o j e", j=PACK, e=2)[:, :, :, halves]
+                kept = slice(wanted[0], wanted[-1] + 1)
+                dst = grouped_k[:, 2 * w : 2 * w + 2].rearrange("p e o j -> p o j e")[:, :, :, kept]
+                src = turned[:].bitcast(BF16).rearrange("p (j o e) -> p o j e", j=PACK, e=2)[:, :, :, kept]
                 if w % 3 == 0:
                     nc.vector.tensor_copy(out=dst, in_=src)
                 else:
                     nc.scalar.copy(out=dst, in_=src)
-            quantise_kernel(c, grouped_k)
 
-        def kernel_in_short_runs(c, chunk_pool, grouped_k):
-            channels = slice(c * K_PASS, (c + 1) * K_PASS)
-            for chunk in range(COUT // O_CHUNK):
-                o_range = slice(chunk * O_CHUNK, (chunk + 1) * O_CHUNK)
-                raw_k = chunk_pool.tile([P, O_CHUNK, PACK * TAPS_ALL], BF16)
-                nc.sync.dma_start(
-                    out=raw_k[:],
-                    in_=kernel[o_range, channels].rearrange("o (p j) f m n -> p o (j f m n)", j=PACK),
-                )
-                for first in range(0, TAPS_ALL, TAPS_PER_COPY):
-                    four_taps = slice(first, first + TAPS_PER_COPY)
-                    dst = grouped_k[:, four_taps, o_range, :].rearrange("p r o j -> p o j r")
-                    src = raw_k[:].rearrange("p o (j r) -> p o j r", j=PACK)[:, :, :, four_taps]
-                    if chunk % 2 == 0:
-                        nc.scalar.copy(out=dst, in_=src)
-                    else:
-                        nc.vector.tensor_copy(out=dst, in_=src)
-            quantise_kernel(c, grouped_k)
-
-        def load_and_quantise_x(b, c, raw):
-            channels = slice(c * K_PASS, (c + 1) * K_PASS)
+        def load_kernel_chunk(c, chunk):
+            raw_k = chunk_pool.tile([P, O_CHUNK, PACK * TAPS_ALL], BF16, name="raw_k%d" % chunk, tag="raw_k")
             nc.sync.dma_start(
-                out=raw[:, :, PAD : PAD + T, :],
-                in_=x[b, channels].rearrange("(p j) t f -> p j t f", j=PACK),
+                out=raw_k[:],
+                in_=kernel[chunk * O_CHUNK : (chunk + 1) * O_CHUNK, c * K_PASS : (c + 1) * K_PASS].rearrange(
+                    "o (p j) f m n -> p o (j f m n)", j=PACK
+                ),
             )
-            grouped_x = grouped_x_pool.tile([P, F, PLANES, PLANE, PACK], BF16, align_bytes=64)
-            for plane in range(PLANES):
-                first = plane + PAD - 1
-                dst = grouped_x[:, :, plane].rearrange("p f q j -> p q j f")
-                src = raw[:, :, first : first + STEP * (PLANE - 1) + 1 : STEP, :].rearrange("p j q f -> p q j f")
-                if plane % 3 == 2:
+            return raw_k
+
+        def sort_kernel_chunk(chunk, raw_k):
+            for group in range(TAPS_ALL // TAPS_PER_COPY):
+                four_taps = slice(group * TAPS_PER_COPY, (group + 1) * TAPS_PER_COPY)
+                o_range = slice(chunk * O_CHUNK, (chunk + 1) * O_CHUNK)
+                dst = grouped_k[:, four_taps, o_range, :].rearrange("p r o j -> p o j r")
+                src = raw_k[:].rearrange("p o (j r) -> p o j r", j=PACK)[:, :, :, four_taps]
+                if group % 3 == 2:
                     nc.scalar.copy(out=dst, in_=src)
                 else:
                     nc.vector.tensor_copy(out=dst, in_=src)
-            for f in range(F):
-                flat = grouped_x[:, f].rearrange("p l q j -> p (l q j)")
-                for first, width in ((0, 512), (512, 128)):
-                    nc.vector.quantize_mx(
-                        out=x_codes[:, b, c, f, first : first + width].bitcast(FP8X4),
-                        scales=x_scales[:, b, c, f, first : first + width],
-                        in_=flat[:, PACK * first : PACK * (first + width)],
-                    )
 
-        def multiply(b, c, acc):
+        def multiply(b, c, half, acc):
             for slot, (f, m, n) in enumerate(taps):
                 window = slice(m * PLANE, m * PLANE + T)
                 nc.tensor.matmul_mx(
                     out=acc[b][f][:],
-                    lhsT=k_codes[:, c, slot, :].bitcast(FP8X4),
-                    lhsT_scale=k_scales[:, c, slot, :],
-                    rhs=x_codes[:, b, c, f + n - 1, window].bitcast(FP8X4),
-                    rhs_scale=x_scales[:, b, c, f + n - 1, window],
+                    lhsT=half["k_codes"][:, slot, :].bitcast(FP8X4),
+                    lhsT_scale=half["k_scales"][:, slot, :],
+                    rhs=half["x_codes"][:, b, f + n - 1, window].bitcast(FP8X4),
+                    rhs_scale=half["x_scales"][:, b, f + n - 1, window],
                     start=(c == 0 and (slot == 0 or taps[slot - 1][0] != f)),
                     stop=(c == HALVES - 1 and (slot == len(taps) - 1 or taps[slot + 1][0] != f)),
                 )
 
-        def store(b, acc, by_bin, result):
+        def store(b, acc):
+            results = raw_x_pool.tile([P, 2, F * T], F32, name="results%d" % b, tag="raw_x")
+            by_bin = results[:, 0, :].rearrange("p (f t) -> p f t", f=F)
+            by_frame = results[:, 1, :].rearrange("p (t f) -> p t f", f=F)
             for f in range(F):
                 nc.scalar.activation(
                     out=by_bin[:, f, :].rearrange("p (q r) -> p q r", r=STEP),
@@ -150,29 +159,36 @@ def tile_svconv2d_pa_t_kernel(tc, x, kernel, bias, out):
                     func=mybir.ActivationFunctionType.Identity,
                     bias=bias_f32[:, f : f + 1],
                 )
-            nc.vector.tensor_copy(out=result[:], in_=by_bin[:].rearrange("p f t -> p t f"))
-            nc.sync.dma_start(out=out[b].rearrange("o t f -> o (t f)"), in_=result[:].rearrange("p t f -> p (t f)"))
+            nc.vector.tensor_copy(out=by_frame, in_=by_bin.rearrange("p f t -> p t f"))
+            nc.sync.dma_start(out=out[b].rearrange("o t f -> o (t f)"), in_=results[:, 1, :])
 
-        with tc.tile_pool(name="grouped_k", bufs=1) as grouped_k_pool:
-            grouped_k = grouped_k_pool.tile([P, TAPS_ALL, COUT, PACK], BF16, align_bytes=64)
-            load_and_quantise_x(0, 0, raw_x[0])
-            with tc.tile_pool(name="whole", bufs=1) as whole_pool:
-                kernel_by_transposes(0, whole_pool, grouped_k)
-            load_and_quantise_x(1, 0, raw_x[1])
-            acc = [
-                [psum.tile([P, T], F32, name="acc_%d_%d" % (b, f), tag="bank%d" % (b * F + f)) for f in range(F)]
-                for b in range(B)
-            ]
-            multiply(0, 0, acc)
-            multiply(1, 0, acc)
-            load_and_quantise_x(0, 1, raw_x[0])
-            with tc.tile_pool(name="chunks", bufs=3) as chunk_pool:
-                kernel_in_short_runs(1, chunk_pool, grouped_k)
-        load_and_quantise_x(1, 1, raw_x[1])
-        with tc.tile_pool(name="results", bufs=1) as results:
-            by_bin = results.tile([P, F, T], F32)
-            result = results.tile([P, T, F], F32)
-            multiply(0, 1, acc)
-            store(0, acc, by_bin, result)
-            multiply(1, 1, acc)
-            store(1, acc, by_bin, result)
+        first_half = quantised_half(keep, 0)
+        raw_0_0 = load_x(0, 0)
+        raw_1_0 = load_x(1, 0)
+        with tc.tile_pool(name="by_output", bufs=1) as by_output_pool:
+            by_output = by_output_pool.tile([P, K_PASS * TAPS_ALL], BF16)
+            nc.sync.dma_start(out=by_output[:], in_=kernel[:, 0:K_PASS].rearrange("o i f m n -> o (i f m n)"))
+            quantise_x(0, raw_0_0, first_half)
+            quantise_x(1, raw_1_0, first_half)
+            raw_0_1 = load_x(0, 1)
+            chunks = [load_kernel_chunk(1, chunk) for chunk in range(COUT // O_CHUNK)]
+            raw_1_1 = load_x(1, 1)
+            turn_kernel(by_output)
+            quantise_kernel(first_half)
+        second_half = quantised_half(ctx.enter_context(tc.tile_pool(name="second_half", bufs=1)), 1)
+
+        acc = [
+            [psum.tile([P, T], F32, name="acc_%d_%d" % (b, f), tag="bank%d" % (b * F + f)) for f in range(F)]
+            for b in range(B)
+        ]
+        multiply(0, 0, first_half, acc)
+        multiply(1, 0, first_half, acc)
+        quantise_x(0, raw_0_1, second_half)
+        for chunk, raw_k in enumerate(chunks):
+            sort_kernel_chunk(chunk, raw_k)
+        quantise_kernel(second_half)
+        quantise_x(1, raw_1_1, second_half)
+        multiply(0, 1, second_half, acc)
+        store(0, acc)
+        multiply(1, 1, second_half, acc)
+        store(1, acc)

@@ -24,6 +24,8 @@ PLANES = STEP + KH - 1
 PAD = 4
 FRAMES = PAD + T + PAD
 
+X_ORDER = ("(j p) t f -> p j t f", "(p j) t f -> p j t f")
+QUARTER = P * TAPS_ALL
 O_CHUNK = 32
 TAPS_PER_COPY = 4
 
@@ -68,7 +70,7 @@ def tile_svconv2d_pa_t_kernel(tc, x, kernel, bias, out):
             nc.vector.memset(raw[:, :, PAD + T : FRAMES, :], 0.0)
             nc.sync.dma_start(
                 out=raw[:, :, PAD : PAD + T, :],
-                in_=x[b, c * K_PASS : (c + 1) * K_PASS].rearrange("(p j) t f -> p j t f", j=PACK),
+                in_=x[b, c * K_PASS : (c + 1) * K_PASS].rearrange(X_ORDER[c], j=PACK),
             )
             return raw
 
@@ -100,11 +102,22 @@ def tile_svconv2d_pa_t_kernel(tc, x, kernel, bias, out):
                 )
 
         def turn_kernel(by_output):
-            words = by_output[:].bitcast(F32).rearrange("o (p j w) -> o p j w", j=PACK, w=TAP_PAIRS)
+            words = by_output[:].bitcast(F32).rearrange("o (j p w) -> o j p w", j=PACK, w=TAP_PAIRS)
+
+            def turn(turned, w, j):
+                nc.tensor.transpose(turned[:, j * COUT : (j + 1) * COUT], words[:, j, :, w], identity[:])
+
+            early = [psum.tile([P, PACK * COUT], F32, name="turned%d" % w, tag="bank%d" % w) for w in range(BANKS)]
+            for j in range(PACK):
+                for w in range(BANKS):
+                    turn(early[w], w, j)
             for w in range(TAP_PAIRS):
-                turned = psum.tile([P, PACK * COUT], F32, name="turned%d" % w, tag="bank%d" % (w % BANKS))
-                for j in range(PACK):
-                    nc.tensor.transpose(turned[:, j * COUT : (j + 1) * COUT], words[:, :, j, w], identity[:])
+                if w < BANKS:
+                    turned = early[w]
+                else:
+                    turned = psum.tile([P, PACK * COUT], F32, name="turned%d" % w, tag="bank%d" % (w % BANKS))
+                    for j in range(PACK):
+                        turn(turned, w, j)
                 wanted = [e for e in range(2) if 2 * w + e in places]
                 kept = slice(wanted[0], wanted[-1] + 1)
                 dst = grouped_k[:, 2 * w : 2 * w + 2].rearrange("p e o j -> p o j e")[:, :, :, kept]
@@ -152,22 +165,35 @@ def tile_svconv2d_pa_t_kernel(tc, x, kernel, bias, out):
             results = raw_x_pool.tile([P, 2, F * T], F32, name="results%d" % b, tag="raw_x")
             by_bin = results[:, 0, :].rearrange("p (f t) -> p f t", f=F)
             by_frame = results[:, 1, :].rearrange("p (t f) -> p t f", f=F)
-            for f in range(F):
+            def leave_psum(f, first_q, last_q):
                 nc.scalar.activation(
-                    out=by_bin[:, f, :].rearrange("p (q r) -> p q r", r=STEP),
-                    in_=acc[b][f][:].rearrange("p (r q) -> p q r", r=STEP),
+                    out=by_bin[:, f, first_q * STEP : last_q * STEP].rearrange("p (q r) -> p q r", r=STEP),
+                    in_=acc[b][f][:].rearrange("p (r q) -> p q r", r=STEP)[:, first_q:last_q, :],
                     func=mybir.ActivationFunctionType.Identity,
                     bias=bias_f32[:, f : f + 1],
                 )
-            nc.vector.tensor_copy(out=by_frame, in_=by_bin.rearrange("p f t -> p t f"))
-            nc.sync.dma_start(out=out[b].rearrange("o t f -> o (t f)"), in_=results[:, 1, :])
+
+            for f in range(F - 1):
+                leave_psum(f, 0, PLANE)
+            for part in range(2):
+                leave_psum(F - 1, part * PLANE // 2, (part + 1) * PLANE // 2)
+                frames = slice(part * T // 2, (part + 1) * T // 2)
+                nc.vector.tensor_copy(out=by_frame[:, frames, :], in_=by_bin[:, :, frames].rearrange("p f t -> p t f"))
+                nc.sync.dma_start(
+                    out=out[b, :, frames, :].rearrange("o t f -> o (t f)"),
+                    in_=by_frame[:, frames, :].rearrange("p t f -> p (t f)"),
+                )
 
         first_half = quantised_half(keep, 0)
         raw_0_0 = load_x(0, 0)
         raw_1_0 = load_x(1, 0)
         with tc.tile_pool(name="by_output", bufs=1) as by_output_pool:
             by_output = by_output_pool.tile([P, K_PASS * TAPS_ALL], BF16)
-            nc.sync.dma_start(out=by_output[:], in_=kernel[:, 0:K_PASS].rearrange("o i f m n -> o (i f m n)"))
+            for quarter in range(PACK):
+                nc.sync.dma_start(
+                    out=by_output[:, quarter * QUARTER : (quarter + 1) * QUARTER],
+                    in_=kernel[:, quarter * P : (quarter + 1) * P].rearrange("o i f m n -> o (i f m n)"),
+                )
             quantise_x(0, raw_0_0, first_half)
             quantise_x(1, raw_1_0, first_half)
             raw_0_1 = load_x(0, 1)

@@ -6,6 +6,7 @@ from concourse.masks import make_identity
 BF16 = mybir.dt.bfloat16
 F32 = mybir.dt.float32
 U32 = mybir.dt.uint32
+I32 = mybir.dt.int32
 U8 = mybir.dt.uint8
 FP8X4 = mybir.dt.float8_e4m3fn_x4
 
@@ -37,6 +38,7 @@ def tile_svconv2d_pa_t_kernel(tc, x, kernel, bias, out):
 
     taps = [(f, m, n) for f in range(F) for m in range(KH) for n in range(KW) if 0 <= f + n - 1 < F]
     places = [(f * KH + m) * KW + n for f, m, n in taps]
+    order = sorted(range(len(taps)), key=lambda slot: (taps[slot][0], taps[slot][1] != 1, slot))
 
     with ExitStack() as ctx:
         keep = ctx.enter_context(tc.tile_pool(name="keep", bufs=1))
@@ -50,9 +52,15 @@ def tile_svconv2d_pa_t_kernel(tc, x, kernel, bias, out):
             return {
                 "k_codes": pool.tile([P, len(taps), COUT], U32, name="k_codes%d" % c, align_bytes=64),
                 "k_scales": pool.tile([P, len(taps), COUT], U8, name="k_scales%d" % c, align_bytes=64),
-                "x_codes": pool.tile([P, B, F, PLANES * PLANE], U32, name="x_codes%d" % c, align_bytes=64),
-                "x_scales": pool.tile([P, B, F, PLANES * PLANE], U8, name="x_scales%d" % c, align_bytes=64),
+                "x_codes": pool.tile([P, B, F, PLANES * PLANE], I32, name="x_codes%d" % c, align_bytes=64),
+                "x_scales": keep.tile([P, B, F, PLANES * PLANE], U8, name="x_scales%d" % c, align_bytes=64),
             }
+
+        def zero_frames(half, scales_too):
+            nc.vector.memset(half["x_codes"][:, :, :, 0:1], 0)
+            nc.vector.memset(half["x_codes"][:, :, :, PLANES * PLANE - 1 : PLANES * PLANE], 0)
+            if scales_too:
+                nc.vector.memset(half["x_scales"][:].rearrange("p b f w -> p (b f w)").bitcast(I32), 0)
 
         grouped_k = grouped_k_pool.tile([P, TAPS_ALL, COUT, PACK], BF16, align_bytes=64)
 
@@ -65,40 +73,42 @@ def tile_svconv2d_pa_t_kernel(tc, x, kernel, bias, out):
         nc.vector.tensor_copy(out=bias_f32[:], in_=bias_bf16[:])
 
         def load_x(b, c):
-            raw = raw_x_pool.tile([P, PACK, FRAMES, F], BF16, name="raw_x_%d_%d" % (b, c), tag="raw_x")
-            nc.vector.memset(raw[:, :, 0:PAD, :], 0.0)
-            nc.vector.memset(raw[:, :, PAD + T : FRAMES, :], 0.0)
+            raw = raw_x_pool.tile([P, PACK, T, F], BF16, name="raw_x_%d_%d" % (b, c), tag="raw_x")
             nc.sync.dma_start(
-                out=raw[:, :, PAD : PAD + T, :],
+                out=raw[:],
                 in_=x[b, c * K_PASS : (c + 1) * K_PASS].rearrange(X_ORDER[c], j=PACK),
             )
             return raw
 
         def quantise_x(b, raw, half):
-            grouped_x = grouped_x_pool.tile([P, F, PLANES, PLANE, PACK], BF16, align_bytes=64)
-            for plane in range(PLANES):
-                first = plane + PAD - 1
-                dst = grouped_x[:, :, plane].rearrange("p f q j -> p q j f")
-                src = raw[:, :, first : first + STEP * (PLANE - 1) + 1 : STEP, :].rearrange("p j q f -> p q j f")
-                if plane % 2 == 0:
+            grouped_x = grouped_x_pool.tile([P, F, STEP, PLANE, PACK], BF16, align_bytes=64)
+            for r in range(STEP):
+                dst = grouped_x[:, :, r].rearrange("p f q j -> p q j f")
+                src = raw[:, :, r : r + STEP * (PLANE - 1) + 1 : STEP, :].rearrange("p j q f -> p q j f")
+                if r % 2 == 1:
                     nc.vector.tensor_copy(out=dst, in_=src)
                 else:
                     nc.scalar.copy(out=dst, in_=src)
+            true_planes = slice(PLANE, (STEP + 1) * PLANE)
             for f in range(F):
-                flat = grouped_x[:, f].rearrange("p l q j -> p (l q j)")
-                for first, width in ((0, 512), (512, 128)):
-                    nc.vector.quantize_mx(
-                        out=half["x_codes"][:, b, f, first : first + width].bitcast(FP8X4),
-                        scales=half["x_scales"][:, b, f, first : first + width],
-                        in_=flat[:, PACK * first : PACK * (first + width)],
-                    )
+                nc.vector.quantize_mx(
+                    out=half["x_codes"][:, b, f, true_planes].bitcast(FP8X4),
+                    scales=half["x_scales"][:, b, f, true_planes],
+                    in_=grouped_x[:, f].rearrange("p l q j -> p (l q j)"),
+                )
+            for name in ("x_codes", "x_scales"):
+                whole = half[name][:, b]
+                nc.vector.tensor_copy(out=whole[:, :, 1:PLANE], in_=whole[:, :, STEP * PLANE : (STEP + 1) * PLANE - 1])
+                nc.vector.tensor_copy(
+                    out=whole[:, :, (STEP + 1) * PLANE : PLANES * PLANE - 1], in_=whole[:, :, PLANE + 1 : 2 * PLANE]
+                )
 
-        def quantise_kernel(half):
-            for slot, place in enumerate(places):
+        def quantise_kernel(half, slots=order):
+            for slot in slots:
                 nc.vector.quantize_mx(
                     out=half["k_codes"][:, slot, :].bitcast(FP8X4),
                     scales=half["k_scales"][:, slot, :],
-                    in_=grouped_k[:, place].rearrange("p o j -> p (o j)"),
+                    in_=grouped_k[:, places[slot]].rearrange("p o j -> p (o j)"),
                 )
 
         def turn_kernel(by_output):
@@ -139,17 +149,36 @@ def tile_svconv2d_pa_t_kernel(tc, x, kernel, bias, out):
 
         def sort_kernel_chunk(chunk, raw_k):
             for group in range(TAPS_ALL // TAPS_PER_COPY):
-                four_taps = slice(group * TAPS_PER_COPY, (group + 1) * TAPS_PER_COPY)
-                o_range = slice(chunk * O_CHUNK, (chunk + 1) * O_CHUNK)
-                dst = grouped_k[:, four_taps, o_range, :].rearrange("p r o j -> p o j r")
-                src = raw_k[:].rearrange("p o (j r) -> p o j r", j=PACK)[:, :, :, four_taps]
-                if group % 3 == 2:
-                    nc.scalar.copy(out=dst, in_=src)
-                else:
-                    nc.vector.tensor_copy(out=dst, in_=src)
+                sort_group(chunk, raw_k, group)
+
+        def sort_group(chunk, raw_k, group):
+            four_taps = slice(group * TAPS_PER_COPY, (group + 1) * TAPS_PER_COPY)
+            o_range = slice(chunk * O_CHUNK, (chunk + 1) * O_CHUNK)
+            dst = grouped_k[:, four_taps, o_range, :].rearrange("p r o j -> p o j r")
+            src = raw_k[:].rearrange("p o (j r) -> p o j r", j=PACK)[:, :, :, four_taps]
+            if group % 3 == 2:
+                nc.scalar.copy(out=dst, in_=src)
+            else:
+                nc.vector.tensor_copy(out=dst, in_=src)
+
+        def sort_and_quantise(chunk, raw_k, half):
+            done = [group for group in range(TAPS_ALL // TAPS_PER_COPY) if group % 3 == 2]
+            for group in done:
+                sort_group(chunk, raw_k, group)
+            waiting = []
+            for slot in order:
+                group = places[slot] // TAPS_PER_COPY
+                if group not in done:
+                    sort_group(chunk, raw_k, group)
+                    done.append(group)
+                    quantise_kernel(half, waiting)
+                    waiting = []
+                waiting.append(slot)
+            quantise_kernel(half, waiting)
 
         def multiply(b, c, half, acc):
-            for slot, (f, m, n) in enumerate(taps):
+            for place_in_order, slot in enumerate(order):
+                f, m, n = taps[slot]
                 window = slice(m * PLANE, m * PLANE + T)
                 nc.tensor.matmul_mx(
                     out=acc[b][f][:],
@@ -157,8 +186,8 @@ def tile_svconv2d_pa_t_kernel(tc, x, kernel, bias, out):
                     lhsT_scale=half["k_scales"][:, slot, :],
                     rhs=half["x_codes"][:, b, f + n - 1, window].bitcast(FP8X4),
                     rhs_scale=half["x_scales"][:, b, f + n - 1, window],
-                    start=(c == 0 and (slot == 0 or taps[slot - 1][0] != f)),
-                    stop=(c == HALVES - 1 and (slot == len(taps) - 1 or taps[slot + 1][0] != f)),
+                    start=(c == 0 and (place_in_order == 0 or taps[order[place_in_order - 1]][0] != f)),
+                    stop=(c == HALVES - 1 and (place_in_order == len(order) - 1 or taps[order[place_in_order + 1]][0] != f)),
                 )
 
         def store(b, acc):
@@ -185,6 +214,7 @@ def tile_svconv2d_pa_t_kernel(tc, x, kernel, bias, out):
                 )
 
         first_half = quantised_half(keep, 0)
+        zero_frames(first_half, True)
         raw_0_0 = load_x(0, 0)
         raw_1_0 = load_x(1, 0)
         with tc.tile_pool(name="by_output", bufs=1) as by_output_pool:
@@ -202,6 +232,7 @@ def tile_svconv2d_pa_t_kernel(tc, x, kernel, bias, out):
             turn_kernel(by_output)
             quantise_kernel(first_half)
         second_half = quantised_half(ctx.enter_context(tc.tile_pool(name="second_half", bufs=1)), 1)
+        zero_frames(second_half, True)
 
         acc = [
             [psum.tile([P, T], F32, name="acc_%d_%d" % (b, f), tag="bank%d" % (b * F + f)) for f in range(F)]
@@ -210,9 +241,9 @@ def tile_svconv2d_pa_t_kernel(tc, x, kernel, bias, out):
         multiply(0, 0, first_half, acc)
         multiply(1, 0, first_half, acc)
         quantise_x(0, raw_0_1, second_half)
-        for chunk, raw_k in enumerate(chunks):
+        for chunk, raw_k in enumerate(chunks[:-1]):
             sort_kernel_chunk(chunk, raw_k)
-        quantise_kernel(second_half)
+        sort_and_quantise(len(chunks) - 1, chunks[-1], second_half)
         quantise_x(1, raw_1_1, second_half)
         multiply(0, 1, second_half, acc)
         store(0, acc)

@@ -27,6 +27,7 @@ FRAMES = PAD + T + PAD
 
 X_ORDER = ("(j p) t f -> p j t f", "(p j) t f -> p j t f")
 QUARTER = P * TAPS_ALL
+SCALAR_FROM = 4
 O_CHUNK = 32
 TAPS_PER_COPY = 4
 
@@ -85,7 +86,7 @@ def tile_svconv2d_pa_t_kernel(tc, x, kernel, bias, out):
             for r in range(STEP):
                 dst = grouped_x[:, :, r].rearrange("p f q j -> p q j f")
                 src = raw[:, :, r : r + STEP * (PLANE - 1) + 1 : STEP, :].rearrange("p j q f -> p q j f")
-                if r % 2 == 1:
+                if r % 3 != 1:
                     nc.vector.tensor_copy(out=dst, in_=src)
                 else:
                     nc.scalar.copy(out=dst, in_=src)
@@ -149,27 +150,28 @@ def tile_svconv2d_pa_t_kernel(tc, x, kernel, bias, out):
 
         def sort_kernel_chunk(chunk, raw_k):
             for group in range(TAPS_ALL // TAPS_PER_COPY):
-                sort_group(chunk, raw_k, group)
+                sort_group(chunk, raw_k, group, group % 3 == 2)
 
-        def sort_group(chunk, raw_k, group):
-            four_taps = slice(group * TAPS_PER_COPY, (group + 1) * TAPS_PER_COPY)
+        def sort_group(chunk, raw_k, group, on_scalar):
+            wanted = [place for place in places if place // TAPS_PER_COPY == group]
+            four_taps = slice(wanted[0], wanted[-1] + 1)
             o_range = slice(chunk * O_CHUNK, (chunk + 1) * O_CHUNK)
             dst = grouped_k[:, four_taps, o_range, :].rearrange("p r o j -> p o j r")
             src = raw_k[:].rearrange("p o (j r) -> p o j r", j=PACK)[:, :, :, four_taps]
-            if group % 3 == 2:
+            if on_scalar:
                 nc.scalar.copy(out=dst, in_=src)
             else:
                 nc.vector.tensor_copy(out=dst, in_=src)
 
         def sort_and_quantise(chunk, raw_k, half):
-            done = [group for group in range(TAPS_ALL // TAPS_PER_COPY) if group % 3 == 2]
+            done = list(range(SCALAR_FROM, TAPS_ALL // TAPS_PER_COPY))
             for group in done:
-                sort_group(chunk, raw_k, group)
+                sort_group(chunk, raw_k, group, True)
             waiting = []
             for slot in order:
                 group = places[slot] // TAPS_PER_COPY
                 if group not in done:
-                    sort_group(chunk, raw_k, group)
+                    sort_group(chunk, raw_k, group, False)
                     done.append(group)
                     quantise_kernel(half, waiting)
                     waiting = []

from contextlib import ExitStack

import concourse.mybir as mybir
from concourse.masks import make_identity

BF16 = mybir.dt.bfloat16
F32 = mybir.dt.float32
U32 = mybir.dt.uint32
I32 = mybir.dt.int32
U8 = mybir.dt.uint8
FP8X4 = mybir.dt.float8_e4m3fn_x4

B, CIN, COUT, T, F, KH, KW = 2, 1024, 128, 512, 4, 3, 3
P = 128
PACK = 4
K_PASS = P * PACK
HALVES = CIN // K_PASS
TAPS_ALL = F * KH * KW
TAP_PAIRS = TAPS_ALL // 2
BANKS = 8

PLANE = 64
STEP = T // PLANE
PLANES = STEP + KH - 1
PAD = 4
FRAMES = PAD + T + PAD

X_ORDER = ("(j p) t f -> p j t f", "(p j) t f -> p j t f")
QUARTER = P * TAPS_ALL
SCALAR_FROM = 4
O_CHUNK = 32
TAPS_PER_COPY = 4

FLOPS = 2 * 30 * B * T * CIN * COUT


def tile_svconv2d_pa_t_kernel(tc, x, kernel, bias, out):
    nc = tc.nc

    taps = [(f, m, n) for f in range(F) for m in range(KH) for n in range(KW) if 0 <= f + n - 1 < F]
    places = [(f * KH + m) * KW + n for f, m, n in taps]
    order = sorted(range(len(taps)), key=lambda slot: (taps[slot][0], taps[slot][1] != 1, slot))

    with ExitStack() as ctx:
        keep = ctx.enter_context(tc.tile_pool(name="keep", bufs=1))
        raw_x_pool = ctx.enter_context(tc.tile_pool(name="raw_x", bufs=2))
        grouped_x_pool = ctx.enter_context(tc.tile_pool(name="grouped_x", bufs=2))
        grouped_k_pool = ctx.enter_context(tc.tile_pool(name="grouped_k", bufs=1))
        chunk_pool = ctx.enter_context(tc.tile_pool(name="chunks", bufs=COUT // O_CHUNK))
        psum = ctx.enter_context(tc.psum_pool(name="psum", bufs=1))

        def quantised_half(pool, c):
            return {
                "k_codes": pool.tile([P, len(taps), COUT], U32, name="k_codes%d" % c, align_bytes=64),
                "k_scales": pool.tile([P, len(taps), COUT], U8, name="k_scales%d" % c, align_bytes=64),
                "x_codes": pool.tile([P, B, F, PLANES * PLANE], I32, name="x_codes%d" % c, align_bytes=64),
                "x_scales": keep.tile([P, B, F, PLANES * PLANE], U8, name="x_scales%d" % c, align_bytes=64),
            }

        def zero_frames(half, scales_too):
            nc.vector.memset(half["x_codes"][:, :, :, 0:1], 0)
            nc.vector.memset(half["x_codes"][:, :, :, PLANES * PLANE - 1 : PLANES * PLANE], 0)
            if scales_too:
                nc.vector.memset(half["x_scales"][:].rearrange("p b f w -> p (b f w)").bitcast(I32), 0)

        grouped_k = grouped_k_pool.tile([P, TAPS_ALL, COUT, PACK], BF16, align_bytes=64)

        identity = keep.tile([P, P], F32)
        make_identity(nc, identity[:])

        bias_bf16 = keep.tile([P, F], BF16)
        nc.scalar.dma_start(out=bias_bf16[:], in_=bias[0, :, 0, :])
        bias_f32 = keep.tile([P, F], F32)
        nc.vector.tensor_copy(out=bias_f32[:], in_=bias_bf16[:])

        def load_x(b, c):
            raw = raw_x_pool.tile([P, PACK, T, F], BF16, name="raw_x_%d_%d" % (b, c), tag="raw_x")
            nc.sync.dma_start(
                out=raw[:],
                in_=x[b, c * K_PASS : (c + 1) * K_PASS].rearrange(X_ORDER[c], j=PACK),
            )
            return raw

        def quantise_x(b, raw, half):
            grouped_x = grouped_x_pool.tile([P, F, STEP, PLANE, PACK], BF16, align_bytes=64)
            for r in range(STEP):
                dst = grouped_x[:, :, r].rearrange("p f q j -> p q j f")
                src = raw[:, :, r : r + STEP * (PLANE - 1) + 1 : STEP, :].rearrange("p j q f -> p q j f")
                if r % 3 != 1:
                    nc.vector.tensor_copy(out=dst, in_=src)
                else:
                    nc.scalar.copy(out=dst, in_=src)
            true_planes = slice(PLANE, (STEP + 1) * PLANE)
            for f in range(F):
                nc.vector.quantize_mx(
                    out=half["x_codes"][:, b, f, true_planes].bitcast(FP8X4),
                    scales=half["x_scales"][:, b, f, true_planes],
                    in_=grouped_x[:, f].rearrange("p l q j -> p (l q j)"),
                )
            for name in ("x_codes", "x_scales"):
                whole = half[name][:, b]
                nc.vector.tensor_copy(out=whole[:, :, 1:PLANE], in_=whole[:, :, STEP * PLANE : (STEP + 1) * PLANE - 1])
                nc.vector.tensor_copy(
                    out=whole[:, :, (STEP + 1) * PLANE : PLANES * PLANE - 1], in_=whole[:, :, PLANE + 1 : 2 * PLANE]
                )

        def quantise_kernel(half, slots=order):
            for slot in slots:
                nc.vector.quantize_mx(
                    out=half["k_codes"][:, slot, :].bitcast(FP8X4),
                    scales=half["k_scales"][:, slot, :],
                    in_=grouped_k[:, places[slot]].rearrange("p o j -> p (o j)"),
                )

        def turn_kernel(by_output):
            words = by_output[:].bitcast(F32).rearrange("o (j p w) -> o j p w", j=PACK, w=TAP_PAIRS)

            def turn(turned, w, j):
                nc.tensor.transpose(turned[:, j * COUT : (j + 1) * COUT], words[:, j, :, w], identity[:])

            early = [psum.tile([P, PACK * COUT], F32, name="turned%d" % w, tag="bank%d" % w) for w in range(BANKS)]
            for j in range(PACK):
                for w in range(BANKS):
                    turn(early[w], w, j)
            for w in range(TAP_PAIRS):
                if w < BANKS:
                    turned = early[w]
                else:
                    turned = psum.tile([P, PACK * COUT], F32, name="turned%d" % w, tag="bank%d" % (w % BANKS))
                    for j in range(PACK):
                        turn(turned, w, j)
                wanted = [e for e in range(2) if 2 * w + e in places]
                kept = slice(wanted[0], wanted[-1] + 1)
                dst = grouped_k[:, 2 * w : 2 * w + 2].rearrange("p e o j -> p o j e")[:, :, :, kept]
                src = turned[:].bitcast(BF16).rearrange("p (j o e) -> p o j e", j=PACK, e=2)[:, :, :, kept]
                if w % 3 == 0:
                    nc.vector.tensor_copy(out=dst, in_=src)
                else:
                    nc.scalar.copy(out=dst, in_=src)

        def load_kernel_chunk(c, chunk):
            raw_k = chunk_pool.tile([P, O_CHUNK, PACK * TAPS_ALL], BF16, name="raw_k%d" % chunk, tag="raw_k")
            nc.sync.dma_start(
                out=raw_k[:],
                in_=kernel[chunk * O_CHUNK : (chunk + 1) * O_CHUNK, c * K_PASS : (c + 1) * K_PASS].rearrange(
                    "o (p j) f m n -> p o (j f m n)", j=PACK
                ),
            )
            return raw_k

        def sort_kernel_chunk(chunk, raw_k):
            for group in range(TAPS_ALL // TAPS_PER_COPY):
                sort_group(chunk, raw_k, group, group % 3 == 2)

        def sort_group(chunk, raw_k, group, on_scalar):
            wanted = [place for place in places if place // TAPS_PER_COPY == group]
            four_taps = slice(wanted[0], wanted[-1] + 1)
            o_range = slice(chunk * O_CHUNK, (chunk + 1) * O_CHUNK)
            dst = grouped_k[:, four_taps, o_range, :].rearrange("p r o j -> p o j r")
            src = raw_k[:].rearrange("p o (j r) -> p o j r", j=PACK)[:, :, :, four_taps]
            if on_scalar:
                nc.scalar.copy(out=dst, in_=src)
            else:
                nc.vector.tensor_copy(out=dst, in_=src)

        def sort_and_quantise(chunk, raw_k, half):
            done = list(range(SCALAR_FROM, TAPS_ALL // TAPS_PER_COPY))
            for group in done:
                sort_group(chunk, raw_k, group, True)
            waiting = []
            for slot in order:
                group = places[slot] // TAPS_PER_COPY
                if group not in done:
                    sort_group(chunk, raw_k, group, False)
                    done.append(group)
                    quantise_kernel(half, waiting)
                    waiting = []
                waiting.append(slot)
            quantise_kernel(half, waiting)

        def multiply(b, c, half, acc):
            for place_in_order, slot in enumerate(order):
                f, m, n = taps[slot]
                window = slice(m * PLANE, m * PLANE + T)
                nc.tensor.matmul_mx(
                    out=acc[b][f][:],
                    lhsT=half["k_codes"][:, slot, :].bitcast(FP8X4),
                    lhsT_scale=half["k_scales"][:, slot, :],
                    rhs=half["x_codes"][:, b, f + n - 1, window].bitcast(FP8X4),
                    rhs_scale=half["x_scales"][:, b, f + n - 1, window],
                    start=(c == 0 and (place_in_order == 0 or taps[order[place_in_order - 1]][0] != f)),
                    stop=(c == HALVES - 1 and (place_in_order == len(order) - 1 or taps[order[place_in_order + 1]][0] != f)),
                )

        def store(b, acc):
            results = raw_x_pool.tile([P, 2, F * T], F32, name="results%d" % b, tag="raw_x")
            by_bin = results[:, 0, :].rearrange("p (f t) -> p f t", f=F)
            by_frame = results[:, 1, :].rearrange("p (t f) -> p t f", f=F)
            def leave_psum(f, first_q, last_q):
                nc.scalar.activation(
                    out=by_bin[:, f, first_q * STEP : last_q * STEP].rearrange("p (q r) -> p q r", r=STEP),
                    in_=acc[b][f][:].rearrange("p (r q) -> p q r", r=STEP)[:, first_q:last_q, :],
                    func=mybir.ActivationFunctionType.Identity,
                    bias=bias_f32[:, f : f + 1],
                )

            for f in range(F - 1):
                leave_psum(f, 0, PLANE)
            for part in range(2):
                leave_psum(F - 1, part * PLANE // 2, (part + 1) * PLANE // 2)
                frames = slice(part * T // 2, (part + 1) * T // 2)
                nc.vector.tensor_copy(out=by_frame[:, frames, :], in_=by_bin[:, :, frames].rearrange("p f t -> p t f"))
                nc.sync.dma_start(
                    out=out[b, :, frames, :].rearrange("o t f -> o (t f)"),
                    in_=by_frame[:, frames, :].rearrange("p t f -> p (t f)"),
                )

        first_half = quantised_half(keep, 0)
        zero_frames(first_half, True)
        raw_0_0 = load_x(0, 0)
        raw_1_0 = load_x(1, 0)
        with tc.tile_pool(name="by_output", bufs=1) as by_output_pool:
            by_output = by_output_pool.tile([P, K_PASS * TAPS_ALL], BF16)
            for quarter in range(PACK):
                nc.sync.dma_start(
                    out=by_output[:, quarter * QUARTER : (quarter + 1) * QUARTER],
                    in_=kernel[:, quarter * P : (quarter + 1) * P].rearrange("o i f m n -> o (i f m n)"),
                )
            quantise_x(0, raw_0_0, first_half)
            quantise_x(1, raw_1_0, first_half)
            raw_0_1 = load_x(0, 1)
            chunks = [load_kernel_chunk(1, chunk) for chunk in range(COUT // O_CHUNK)]
            raw_1_1 = load_x(1, 1)
            turn_kernel(by_output)
            quantise_kernel(first_half)
        second_half = quantised_half(ctx.enter_context(tc.tile_pool(name="second_half", bufs=1)), 1)
        zero_frames(second_half, True)

        acc = [
            [psum.tile([P, T], F32, name="acc_%d_%d" % (b, f), tag="bank%d" % (b * F + f)) for f in range(F)]
            for b in range(B)
        ]
        multiply(0, 0, first_half, acc)
        multiply(1, 0, first_half, acc)
        quantise_x(0, raw_0_1, second_half)
        for chunk, raw_k in enumerate(chunks[:-1]):
            sort_kernel_chunk(chunk, raw_k)
        sort_and_quantise(len(chunks) - 1, chunks[-1], second_half)
        quantise_x(1, raw_1_1, second_half)
        multiply(0, 1, second_half, acc)
        store(0, acc)
        multiply(1, 1, second_half, acc)
        store(1, acc)
